import numpy as np
import ml_dtypes


def mxq(x, axis, fmt="e4m3"):
    dtype, down = {"e4m3": (ml_dtypes.float8_e4m3fn, 7), "e5m2": (ml_dtypes.float8_e5m2, 14)}[fmt]
    v = np.moveaxis(np.asarray(x, np.float32).astype(ml_dtypes.bfloat16).astype(np.float64), axis, -1)
    blocks = v.reshape(v.shape[:-1] + (-1, 32))
    amax = np.abs(blocks).max(-1, keepdims=True)
    byte = np.maximum(np.where(amax > 0, np.frexp(amax)[1] - 1 + 127, 0) - down, 1)
    scale = np.exp2(byte - 127.0)
    codes = (blocks / scale).astype(np.float32).astype(dtype).astype(np.float64)
    return np.moveaxis((codes * scale).reshape(v.shape), -1, axis)


WIDE = False


def mx_kscale(k):
    if not WIDE:
        return np.ones(k)
    levels = np.array([10, -10, 5, -5, 0])
    a = np.random.permutation(np.resize(levels, k // 512 * 4)).reshape(k // 512, 4)
    idx = np.arange(k)
    return np.exp2(a[idx // 512, idx % 128 // 32])


BF16 = ml_dtypes.bfloat16


def bf(x):
    return np.asarray(x, np.float32).astype(BF16)


def f64(x):
    return np.asarray(x).astype(np.float64)


B, H, C, W = 1, 512, 4096, 1024
EPS = 1e-8
MASK_MIN = 0.0


def setup_inputs():
    s = mx_kscale(W)
    rows = 0.5 + 1.5 * np.random.random_sample((B, C, 1))
    return {"memory": bf(np.random.standard_normal((B, C, W)) * rows * s),
            "keys": bf(np.random.standard_normal((B, H, W)) * s),
            "betas": bf(np.sqrt(W) * (0.6 + 0.6 * np.random.random_sample((B, H)))),
            "mask": bf(np.random.random_sample((B, H, W)) / s)}


def reference(memory, keys, betas, mask):
    memory, keys, betas = f64(memory), f64(keys), f64(betas)
    mask = f64(mask) * (1.0 - MASK_MIN) + MASK_MIN
    m2 = mask * mask
    keys_m = keys * mask
    dots = mxq(keys * m2, 2, "e4m3") @ mxq(memory, 2, "e4m3").transpose(0, 2, 1)
    keys_norm = np.sqrt((keys_m * keys_m).sum(-1))
    mem_norm = np.sqrt(mxq(m2, 2, "e4m3") @ mxq(memory * memory, 2, "e4m3").transpose(0, 2, 1))
    norm = keys_norm[..., None] * mem_norm
    scores = dots / (norm + EPS) * betas[..., None]
    e = np.exp(scores - scores.max(-1, keepdims=True))
    return e / e.sum(-1, keepdims=True)

@@ -1,0 +1,235 @@
+from contextlib import ExitStack
+
+import concourse.mybir as mybir
+from concourse.masks import make_identity
+
+F32 = mybir.dt.float32
+BF16 = mybir.dt.bfloat16
+U32 = mybir.dt.uint32
+U8 = mybir.dt.uint8
+FP8X4 = mybir.dt.float8_e4m3fn_x4
+AF = mybir.ActivationFunctionType
+ALU = mybir.AluOpType
+AX = mybir.AxisListType
+
+P = 128
+H, C, W = 512, 4096, 1024
+HT = H // P
+CHUNK = 512
+NCH = C // CHUNK
+G = W // 512
+EPS = 1e-8
+FLOPS = 2 * 2 * H * C * W
+
+
+def tile_contentaddressing_t_kernel(tc, memory, keys, betas, mask, out):
+    nc = tc.nc
+    mem2d = memory.flatten_outer_dims()
+    keys2d = keys.flatten_outer_dims()
+    mask2d = mask.flatten_outer_dims()
+    out2d = out.flatten_outer_dims()
+
+    with ExitStack() as ctx:
+        const = ctx.enter_context(tc.tile_pool(name="const", bufs=1))
+        prep = ctx.enter_context(tc.tile_pool(name="prep", bufs=2))
+        natp = ctx.enter_context(tc.tile_pool(name="natp", bufs=3))
+        grp = ctx.enter_context(tc.tile_pool(name="grp", bufs=2))
+        cod = ctx.enter_context(tc.tile_pool(name="cod", bufs=3))
+        wrk = ctx.enter_context(tc.tile_pool(name="wrk", bufs=4))
+        psum = ctx.enter_context(tc.psum_pool(name="psum", bufs=2))
+
+        tiny = const.tile([P, 1], F32, name="tiny")
+        nc.vector.memset(tiny[:], 1e-30)
+        b1 = const.tile([P, 1], F32, name="b1")
+        nc.vector.memset(b1[:], 1e-16)
+        warm = const.tile([P, 1], F32, name="warm")
+        nc.scalar.activation(out=warm[:], in_=b1[:], func=AF.Abs_reciprocal_sqrt, bias=tiny[:], scale=1.0)
+        ident_f = const.tile([P, P], F32, name="ident_f")
+        make_identity(nc, ident_f[:])
+        ident_b = const.tile([P, P], BF16, name="ident_b")
+        make_identity(nc, ident_b[:])
+        brow = const.tile([P, P], BF16, name="brow")
+        nc.vector.memset(brow[:], 0.0)
+
+        keys_nat = const.tile([P, HT, W], BF16, name="keys_nat")
+        mask_nat = const.tile([P, HT, W], BF16, name="mask_nat")
+        kview = keys2d.rearrange("(t p) w -> p t w", p=P)
+        mview = mask2d.rearrange("(t p) w -> p t w", p=P)
+        for half in range(2):
+            sl = slice(2 * half, 2 * half + 2)
+            nc.sync.dma_start(out=mask_nat[:, sl, :], in_=mview[:, sl, :])
+            nc.sync.dma_start(out=keys_nat[:, sl, :], in_=kview[:, sl, :])
+        nc.scalar.dma_start(out=brow[0:HT, :], in_=betas.rearrange("o (t p) -> (o t) p", p=P))
+
+        nat = {}
+
+        def load_mem(k):
+            t_nat = natp.tile([P, 4, W], BF16, name="mem_nat")
+            nc.sync.dma_start(
+                out=t_nat[:],
+                in_=mem2d[k * CHUNK:(k + 1) * CHUNK, :].rearrange("(j p) w -> p j w", p=P),
+            )
+            nat[k] = t_nat
+
+        load_mem(0)
+        load_mem(1)
+
+        bT = psum.tile([P, P], BF16, name="bT", tag="T", bufs=4)
+        nc.tensor.transpose(out=bT[:], in_=brow[:], identity=ident_b[:])
+        beta_f = const.tile([P, HT], F32, name="beta_f")
+        nc.vector.tensor_copy(out=beta_f[:], in_=bT[:, 0:HT])
+
+        kn2 = const.tile([P, HT], F32, name="kn2")
+        rk = const.tile([P, HT], F32, name="rk")
+        rk2 = const.tile([P, HT], F32, name="rk2")
+        sc1 = const.tile([P, HT], F32, name="sc1")
+        e2 = const.tile([P, HT], F32, name="e2")
+        bk = const.tile([P, HT], F32, name="bk")
+        kcodes = const.tile([P, HT * 512], U32, name="kcodes", align_bytes=64)
+        kscale = const.tile([P, HT * 512], U8, name="kscale", align_bytes=64)
+
+        perm = "p (a q e) -> p a e q"
+        for t in range(HT):
+            k_t = keys_nat[:, t, :]
+            m_t = mask_nat[:, t, :]
+            c1 = slice(t, t + 1)
+            m2f = prep.tile([P, W], F32, name="m2f")
+            nc.scalar.activation(out=m2f[:], in_=m_t, func=AF.Square)
+            km2f = prep.tile([P, W], F32, name="km2f")
+            nc.vector.tensor_tensor(out=km2f[:], in0=k_t, in1=m2f[:], op=ALU.mult)
+            junk = prep.tile([P, W], F32, name="junk")
+            nc.vector.scalar_tensor_tensor(out=junk[:], in0=k_t, scalar=1.0, in1=km2f[:],
+                                           op0=ALU.mult, op1=ALU.mult, accum_out=kn2[:, c1])
+            nc.scalar.activation(out=rk[:, c1], in_=kn2[:, c1], func=AF.Abs_reciprocal_sqrt,
+                                 bias=tiny[:], scale=1.0)
+            nc.vector.tensor_scalar(out=sc1[:, c1], in0=kn2[:, c1], scalar1=1.0 / (4.0 * EPS * EPS),
+                                    scalar2=3e38, op0=ALU.mult, op1=ALU.min)
+            nc.vector.tensor_tensor(out=rk2[:, c1], in0=rk[:, c1], in1=rk[:, c1], op=ALU.mult)
+            nc.vector.tensor_scalar(out=e2[:, c1], in0=rk2[:, c1], scalar1=EPS * EPS,
+                                    scalar2=1e-37, op0=ALU.mult, op1=ALU.max)
+            nc.vector.tensor_tensor(out=bk[:, c1], in0=beta_f[:, c1], in1=rk[:, c1], op=ALU.mult)
+
+            kgrp = prep.tile([P, 2, G, P, 4], BF16, name="kgrp", align_bytes=64)
+            for op in range(2):
+                cols = (km2f if op == 0 else m2f)[:].rearrange(perm, a=4, q=P, e=2)
+                for g in range(G):
+                    xt = psum.tile([P, 4, P], F32, name="xt", tag="T", bufs=4)
+                    for u in range(2):
+                        for e in range(2):
+                            nc.tensor.transpose(out=xt[:, 2 * u + e, :], in_=cols[:, 2 * g + u, e, :],
+                                                identity=ident_f[:])
+                    src = xt[:].rearrange("p s h -> p h s")
+                    if g == 0:
+                        nc.vector.tensor_copy(out=kgrp[:, op, g], in_=src)
+                    else:
+                        nc.scalar.copy(out=kgrp[:, op, g], in_=src)
+            nc.vector.quantize_mx(
+                out=kcodes[:, t * 512:(t + 1) * 512].bitcast(FP8X4),
+                scales=kscale[:, t * 512:(t + 1) * 512],
+                in_=kgrp[:].rearrange("p o g h s -> p (o g h s)"),
+            )
+
+        codes = {}
+
+        def mem_prep(k):
+            memf = nat[k][:].bitcast(F32)
+            mgrp = grp.tile([P, G, CHUNK, 4], BF16, name="mgrp", align_bytes=64)
+            msq = grp.tile([P, G, CHUNK, 4], BF16, name="msq", align_bytes=64)
+            mgrp_f = mgrp[:].bitcast(F32)
+            for g in range(G):
+                for half in range(2):
+                    tb = psum.tile([P, 2, 256], F32, name="tb", tag="T", bufs=4)
+                    for jj in range(2):
+                        for u in range(2):
+                            i = 2 * g + u
+                            nc.tensor.transpose(
+                                out=tb[:, u, jj * P:(jj + 1) * P],
+                                in_=memf[:, 2 * half + jj, i * P:(i + 1) * P],
+                                identity=ident_f[:])
+                    cs = slice(256 * half, 256 * half + 256)
+                    nc.scalar.copy(out=mgrp_f[:, g, cs, :], in_=tb[:].rearrange("p u r -> p r u"))
+                    if g == 0:
+                        nc.scalar.activation(
+                            out=msq[:, g, cs, :].rearrange("p r (u e) -> p r u e", e=2),
+                            in_=tb[:].bitcast(BF16).rearrange("p u (r e) -> p r u e", e=2),
+                            func=AF.Square)
+            src = mgrp[:, 1].rearrange("p c s -> p (c s)")
+            nc.vector.tensor_tensor(out=msq[:, 1].rearrange("p c s -> p (c s)"), in0=src, in1=src, op=ALU.mult)
+            mc = cod.tile([P, G * CHUNK], U32, name="mc", align_bytes=64)
+            ms = cod.tile([P, G * CHUNK], U8, name="ms", align_bytes=64)
+            qc = cod.tile([P, G * CHUNK], U32, name="qc", align_bytes=64)
+            qs = cod.tile([P, G * CHUNK], U8, name="qs", align_bytes=64)
+            nc.vector.quantize_mx(out=mc[:].bitcast(FP8X4), scales=ms[:],
+                                  in_=mgrp[:].rearrange("p g c s -> p (g c s)"))
+            nc.vector.quantize_mx(out=qc[:].bitcast(FP8X4), scales=qs[:],
+                                  in_=msq[:].rearrange("p g c s -> p (g c s)"))
+            codes[k] = (mc, ms, qc, qs)
+
+        s_all = [const.tile([P, C], F32, name="s%d" % t) for t in range(HT)]
+        mxp = const.tile([P, NCH], F32, name="mxp")
+
+        def product(acc, t, op, dat, scl):
+            for g in range(G):
+                c0 = t * 512 + (op * G + g) * P
+                nc.tensor.matmul_mx(
+                    out=acc[:],
+                    lhsT=kcodes[:, c0:c0 + P].bitcast(FP8X4),
+                    lhsT_scale=kscale[:, c0:c0 + P],
+                    rhs=dat[:, g * CHUNK:(g + 1) * CHUNK].bitcast(FP8X4),
+                    rhs_scale=scl[:, g * CHUNK:(g + 1) * CHUNK],
+                    start=(g == 0), stop=(g == G - 1))
+
+        def scores(k):
+            mc, ms, qc, qs = codes[k]
+            for t in range(HT):
+                c1 = slice(t, t + 1)
+                mn2 = psum.tile([P, CHUNK], F32, name="mn2")
+                product(mn2, t, 1, qc, qs)
+                dots = psum.tile([P, CHUNK], F32, name="dots")
+                product(dots, t, 0, mc, ms)
+                w = wrk.tile([P, CHUNK], F32, name="w")
+                nc.scalar.activation(out=w[:], in_=mn2[:], func=AF.Abs_reciprocal_sqrt,
+                                     bias=b1[:], scale=sc1[:, c1])
+                nc.vector.scalar_tensor_tensor(out=w[:], in0=w[:], scalar=1.0, in1=mn2[:],
+                                               op0=ALU.add, op1=ALU.mult)
+                nc.scalar.activation(out=w[:], in_=w[:], func=AF.Abs_reciprocal_sqrt,
+                                     bias=e2[:, c1], scale=1.0)
+                sc = s_all[t][:, k * CHUNK:(k + 1) * CHUNK]
+                nc.vector.scalar_tensor_tensor(out=sc, in0=dots[:], scalar=bk[:, c1], in1=w[:],
+                                               op0=ALU.mult, op1=ALU.mult)
+                if t == 0:
+                    nc.vector.tensor_reduce(out=mxp[:, k:k + 1], in_=sc, axis=AX.X, op=ALU.max)
+
+        mem_prep(0)
+        for k in range(NCH):
+            if k + 2 < NCH:
+                load_mem(k + 2)
+            if k + 1 < NCH:
+                mem_prep(k + 1)
+            scores(k)
+
+        for t in range(HT):
+            mrow = const.tile([P, 1], F32, name="mrow%d" % t)
+            nc.vector.tensor_reduce(out=mrow[:], in_=(mxp[:] if t == 0 else s_all[t][:]), axis=AX.X, op=ALU.max)
+            negm = const.tile([P, 1], F32, name="negm%d" % t)
+            nc.vector.tensor_scalar(out=negm[:], in0=mrow[:], scalar1=-1.0, scalar2=None, op0=ALU.mult)
+            sums = const.tile([P, 2], F32, name="sums%d" % t)
+            for i in range(2):
+                cs = slice(i * 2048, (i + 1) * 2048)
+                nc.scalar.activation(out=s_all[t][:, cs], in_=s_all[t][:, cs], func=AF.Exp,
+                                     bias=negm[:], scale=1.0, accum_out=sums[:, i:i + 1])
+            tot = const.tile([P, 1], F32, name="tot%d" % t)
+            nc.vector.tensor_reduce(out=tot[:], in_=sums[:], axis=AX.X, op=ALU.add)
+            rs = const.tile([P, 1], F32, name="rs%d" % t)
+            nc.vector.reciprocal(out=rs[:], in_=tot[:])
+            for q in range(4):
+                cs = slice(q * 1024, (q + 1) * 1024)
+                piece = s_all[t][:, cs]
+                if t == HT - 1 and q < 2:
+                    nc.vector.tensor_scalar(out=piece, in0=piece, scalar1=rs[:], scalar2=None, op0=ALU.mult)
+                elif t == HT - 1 and q == 2:
+                    nc.scalar.activation(out=piece, in_=piece, func=AF.Copy, scale=rs[:])
+                else:
+                    nc.gpsimd.tensor_scalar(out=piece, in0=piece, scalar1=rs[:], scalar2=0.0,
+                                            op0=ALU.mult, op1=ALU.add)
+                nc.sync.dma_start(out=out2d[t * P:(t + 1) * P, cs], in_=piece)

@@ -18,6 +18,8 @@ HT = H // P
 CHUNK = 512
 NCH = C // CHUNK
 G = W // 512
+NPAIR = NCH * HT
+LEAD = 2
 EPS = 1e-8
 FLOPS = 2 * 2 * H * C * W
 
@@ -31,12 +33,12 @@ def tile_contentaddressing_t_kernel(tc, memory, keys, betas, mask, out):
 
     with ExitStack() as ctx:
         const = ctx.enter_context(tc.tile_pool(name="const", bufs=1))
-        prep = ctx.enter_context(tc.tile_pool(name="prep", bufs=2))
         natp = ctx.enter_context(tc.tile_pool(name="natp", bufs=3))
         grp = ctx.enter_context(tc.tile_pool(name="grp", bufs=2))
         cod = ctx.enter_context(tc.tile_pool(name="cod", bufs=3))
         wrk = ctx.enter_context(tc.tile_pool(name="wrk", bufs=4))
         psum = ctx.enter_context(tc.psum_pool(name="psum", bufs=2))
+        ctx.enter_context(tc.manual_schedule())
 
         tiny = const.tile([P, 1], F32, name="tiny")
         nc.vector.memset(tiny[:], 1e-30)
@@ -44,23 +46,17 @@ def tile_contentaddressing_t_kernel(tc, memory, keys, betas, mask, out):
         nc.vector.memset(b1[:], 1e-16)
         warm = const.tile([P, 1], F32, name="warm")
         nc.scalar.activation(out=warm[:], in_=b1[:], func=AF.Abs_reciprocal_sqrt, bias=tiny[:], scale=1.0)
+        brow = const.tile([P, P], BF16, name="brow")
+        nc.vector.memset(brow[:], 0.0)
         ident_f = const.tile([P, P], F32, name="ident_f")
         make_identity(nc, ident_f[:])
         ident_b = const.tile([P, P], BF16, name="ident_b")
         make_identity(nc, ident_b[:])
-        brow = const.tile([P, P], BF16, name="brow")
-        nc.vector.memset(brow[:], 0.0)
 
         keys_nat = const.tile([P, HT, W], BF16, name="keys_nat")
         mask_nat = const.tile([P, HT, W], BF16, name="mask_nat")
         kview = keys2d.rearrange("(t p) w -> p t w", p=P)
         mview = mask2d.rearrange("(t p) w -> p t w", p=P)
-        for half in range(2):
-            sl = slice(2 * half, 2 * half + 2)
-            nc.sync.dma_start(out=mask_nat[:, sl, :], in_=mview[:, sl, :])
-            nc.sync.dma_start(out=keys_nat[:, sl, :], in_=kview[:, sl, :])
-        nc.scalar.dma_start(out=brow[0:HT, :], in_=betas.rearrange("o (t p) -> (o t) p", p=P))
-
         nat = {}
 
         def load_mem(k):
@@ -71,14 +67,15 @@ def tile_contentaddressing_t_kernel(tc, memory, keys, betas, mask, out):
             )
             nat[k] = t_nat
 
+        nc.scalar.dma_start(out=brow[0:HT, :], in_=betas.rearrange("o (t p) -> (o t) p", p=P))
+        for t in range(HT):
+            nc.sync.dma_start(out=mask_nat[:, t, :], in_=mview[:, t, :])
+            nc.sync.dma_start(out=keys_nat[:, t, :], in_=kview[:, t, :])
         load_mem(0)
         load_mem(1)
+        load_mem(2)
 
-        bT = psum.tile([P, P], BF16, name="bT", tag="T", bufs=4)
-        nc.tensor.transpose(out=bT[:], in_=brow[:], identity=ident_b[:])
         beta_f = const.tile([P, HT], F32, name="beta_f")
-        nc.vector.tensor_copy(out=beta_f[:], in_=bT[:, 0:HT])
-
         kn2 = const.tile([P, HT], F32, name="kn2")
         rk = const.tile([P, HT], F32, name="rk")
         rk2 = const.tile([P, HT], F32, name="rk2")
@@ -87,88 +84,110 @@ def tile_contentaddressing_t_kernel(tc, memory, keys, betas, mask, out):
         bk = const.tile([P, HT], F32, name="bk")
         kcodes = const.tile([P, HT * 512], U32, name="kcodes", align_bytes=64)
         kscale = const.tile([P, HT * 512], U8, name="kscale", align_bytes=64)
-
-        perm = "p (a q e) -> p a e q"
-        for t in range(HT):
-            k_t = keys_nat[:, t, :]
-            m_t = mask_nat[:, t, :]
-            c1 = slice(t, t + 1)
-            m2f = prep.tile([P, W], F32, name="m2f")
-            nc.scalar.activation(out=m2f[:], in_=m_t, func=AF.Square)
-            km2f = prep.tile([P, W], F32, name="km2f")
-            nc.vector.tensor_tensor(out=km2f[:], in0=k_t, in1=m2f[:], op=ALU.mult)
-            junk = prep.tile([P, W], F32, name="junk")
-            nc.vector.scalar_tensor_tensor(out=junk[:], in0=k_t, scalar=1.0, in1=km2f[:],
-                                           op0=ALU.mult, op1=ALU.mult, accum_out=kn2[:, c1])
-            nc.scalar.activation(out=rk[:, c1], in_=kn2[:, c1], func=AF.Abs_reciprocal_sqrt,
-                                 bias=tiny[:], scale=1.0)
-            nc.vector.tensor_scalar(out=sc1[:, c1], in0=kn2[:, c1], scalar1=1.0 / (4.0 * EPS * EPS),
-                                    scalar2=3e38, op0=ALU.mult, op1=ALU.min)
-            nc.vector.tensor_tensor(out=rk2[:, c1], in0=rk[:, c1], in1=rk[:, c1], op=ALU.mult)
-            nc.vector.tensor_scalar(out=e2[:, c1], in0=rk2[:, c1], scalar1=EPS * EPS,
-                                    scalar2=1e-37, op0=ALU.mult, op1=ALU.max)
-            nc.vector.tensor_tensor(out=bk[:, c1], in0=beta_f[:, c1], in1=rk[:, c1], op=ALU.mult)
-
-            kgrp = prep.tile([P, 2, G, P, 4], BF16, name="kgrp", align_bytes=64)
-            for op in range(2):
-                cols = (km2f if op == 0 else m2f)[:].rearrange(perm, a=4, q=P, e=2)
-                for g in range(G):
-                    xt = psum.tile([P, 4, P], F32, name="xt", tag="T", bufs=4)
-                    for u in range(2):
-                        for e in range(2):
-                            nc.tensor.transpose(out=xt[:, 2 * u + e, :], in_=cols[:, 2 * g + u, e, :],
-                                                identity=ident_f[:])
-                    src = xt[:].rearrange("p s h -> p h s")
-                    if g == 0:
-                        nc.vector.tensor_copy(out=kgrp[:, op, g], in_=src)
-                    else:
-                        nc.scalar.copy(out=kgrp[:, op, g], in_=src)
-            nc.vector.quantize_mx(
-                out=kcodes[:, t * 512:(t + 1) * 512].bitcast(FP8X4),
-                scales=kscale[:, t * 512:(t + 1) * 512],
-                in_=kgrp[:].rearrange("p o g h s -> p (o g h s)"),
-            )
-
-        codes = {}
-
-        def mem_prep(k):
-            memf = nat[k][:].bitcast(F32)
-            mgrp = grp.tile([P, G, CHUNK, 4], BF16, name="mgrp", align_bytes=64)
-            msq = grp.tile([P, G, CHUNK, 4], BF16, name="msq", align_bytes=64)
-            mgrp_f = mgrp[:].bitcast(F32)
-            for g in range(G):
-                for half in range(2):
-                    tb = psum.tile([P, 2, 256], F32, name="tb", tag="T", bufs=4)
-                    for jj in range(2):
-                        for u in range(2):
-                            i = 2 * g + u
-                            nc.tensor.transpose(
-                                out=tb[:, u, jj * P:(jj + 1) * P],
-                                in_=memf[:, 2 * half + jj, i * P:(i + 1) * P],
-                                identity=ident_f[:])
-                    cs = slice(256 * half, 256 * half + 256)
-                    nc.scalar.copy(out=mgrp_f[:, g, cs, :], in_=tb[:].rearrange("p u r -> p r u"))
-                    if g == 0:
-                        nc.scalar.activation(
-                            out=msq[:, g, cs, :].rearrange("p r (u e) -> p r u e", e=2),
-                            in_=tb[:].bitcast(BF16).rearrange("p u (r e) -> p r u e", e=2),
-                            func=AF.Square)
-            src = mgrp[:, 1].rearrange("p c s -> p (c s)")
-            nc.vector.tensor_tensor(out=msq[:, 1].rearrange("p c s -> p (c s)"), in0=src, in1=src, op=ALU.mult)
-            mc = cod.tile([P, G * CHUNK], U32, name="mc", align_bytes=64)
-            ms = cod.tile([P, G * CHUNK], U8, name="ms", align_bytes=64)
-            qc = cod.tile([P, G * CHUNK], U32, name="qc", align_bytes=64)
-            qs = cod.tile([P, G * CHUNK], U8, name="qs", align_bytes=64)
-            nc.vector.quantize_mx(out=mc[:].bitcast(FP8X4), scales=ms[:],
-                                  in_=mgrp[:].rearrange("p g c s -> p (g c s)"))
-            nc.vector.quantize_mx(out=qc[:].bitcast(FP8X4), scales=qs[:],
-                                  in_=msq[:].rearrange("p g c s -> p (g c s)"))
-            codes[k] = (mc, ms, qc, qs)
-
+        kgrp = [const.tile([P, 2, G, P, 4], BF16, name="kgrp%d" % t, align_bytes=64) for t in range(HT)]
         s_all = [const.tile([P, C], F32, name="s%d" % t) for t in range(HT)]
         mxp = const.tile([P, NCH], F32, name="mxp")
 
-        def product(acc, t, op, dat, scl):
+        def t_bank(shape, dtype):
+            return psum.tile(shape, dtype, name="tbank", tag="T", bufs=3)
+
+        def acc_bank(op, shape):
+            if op == 0:
+                return psum.tile(shape, F32, name="dots", tag="dots", bufs=3)
+            return psum.tile(shape, F32, name="mn2", tag="mn2", bufs=2)
+
+        bT = t_bank([P, P], BF16)
+        nc.tensor.transpose(out=bT[:], in_=brow[:], identity=ident_b[:])
+        nc.vector.tensor_copy(out=beta_f[:], in_=bT[:, 0:HT])
+
+        perm = "p (a q e) -> p a e q"
+        m2f = [s_all[t][:, 0:W] for t in range(HT)]
+        km2f = [s_all[t][:, W:2 * W] for t in range(HT)]
+        junk = [s_all[t][:, 2 * W:3 * W] for t in range(HT)]
+        kx = {}
+
+        def key_square(t):
+            nc.scalar.activation(out=m2f[t], in_=mask_nat[:, t, :], func=AF.Square)
+
+        def key_products(t):
+            k_t = keys_nat[:, t, :]
+            nc.vector.tensor_tensor(out=km2f[t], in0=k_t, in1=m2f[t], op=ALU.mult)
+            nc.vector.scalar_tensor_tensor(out=junk[t], in0=k_t, scalar=1.0, in1=km2f[t],
+                                           op0=ALU.mult, op1=ALU.mult, accum_out=kn2[:, t:t + 1])
+
+        def key_transposes(t, op):
+            cols = (km2f[t] if op == 0 else m2f[t]).rearrange(perm, a=4, q=P, e=2)
+            for g in range(G):
+                xt = acc_bank(g, [P, 4, P])
+                for u in range(2):
+                    for e in range(2):
+                        nc.tensor.transpose(out=xt[:, 2 * u + e, :], in_=cols[:, 2 * g + u, e, :],
+                                            identity=ident_f[:])
+                kx[(t, op, g)] = xt
+
+        def key_evac(t, op, eng):
+            for g in range(G):
+                src = kx[(t, op, g)][:].rearrange("p s h -> p h s")
+                if eng == "v":
+                    nc.vector.tensor_copy(out=kgrp[t][:, op, g], in_=src)
+                else:
+                    nc.scalar.copy(out=kgrp[t][:, op, g], in_=src)
+
+        def key_quant(t):
+            nc.vector.quantize_mx(
+                out=kcodes[:, t * 512:(t + 1) * 512].bitcast(FP8X4),
+                scales=kscale[:, t * 512:(t + 1) * 512],
+                in_=kgrp[t][:].rearrange("p o g h s -> p (o g h s)"),
+            )
+
+        mp = {}
+
+        def mem_transposes(k, b):
+            g, half = divmod(b, 2)
+            memf = nat[k][:].bitcast(F32)
+            tb = t_bank([P, 2, 256], F32)
+            for jj in range(2):
+                for u in range(2):
+                    i = 2 * g + u
+                    nc.tensor.transpose(
+                        out=tb[:, u, jj * P:(jj + 1) * P],
+                        in_=memf[:, 2 * half + jj, i * P:(i + 1) * P],
+                        identity=ident_f[:])
+            mp[(k, "tb", b)] = tb
+
+        def mem_tiles(k):
+            mp[(k, "mgrp")] = grp.tile([P, G, CHUNK, 4], BF16, name="mgrp", align_bytes=64)
+            mp[(k, "msq")] = grp.tile([P, G, CHUNK, 4], BF16, name="msq", align_bytes=64)
+
+        def mem_evac(k, b):
+            g, half = divmod(b, 2)
+            tb = mp[(k, "tb", b)]
+            nc.scalar.copy(out=mp[(k, "mgrp")][:].bitcast(F32)[:, g, 256 * half:256 * half + 256, :],
+                           in_=tb[:].rearrange("p u r -> p r u"))
+            nc.scalar.activation(
+                out=mp[(k, "msq")][:, g, 256 * half:256 * half + P, :].rearrange("p r (u e) -> p r u e", e=2),
+                in_=tb[:, :, 0:P].bitcast(BF16).rearrange("p u (r e) -> p r u e", e=2),
+                func=AF.Square)
+
+        def mem_square_vec(k):
+            view = "p g (h j c) s -> p (g h) j (c s)"
+            src = mp[(k, "mgrp")][:].rearrange(view, h=2, j=2, c=P)[:, :, 1, :]
+            dst = mp[(k, "msq")][:].rearrange(view, h=2, j=2, c=P)[:, :, 1, :]
+            nc.vector.tensor_tensor(out=dst, in0=src, in1=src, op=ALU.mult)
+
+        def quant(k, which):
+            dat = cod.tile([P, G * CHUNK], U32, name="dat_" + which, align_bytes=64)
+            scl = cod.tile([P, G * CHUNK], U8, name="scl_" + which, align_bytes=64)
+            nc.vector.quantize_mx(out=dat[:].bitcast(FP8X4), scales=scl[:],
+                                  in_=mp[(k, which)][:].rearrange("p g c s -> p (g c s)"))
+            mp[(k, "q", which)] = (dat, scl)
+
+        pr = {}
+
+        def product(n, op):
+            k, t = divmod(n, HT)
+            acc = acc_bank(op, [P, CHUNK])
+            dat, scl = mp[(k, "q", "mgrp" if op == 0 else "msq")]
             for g in range(G):
                 c0 = t * 512 + (op * G + g) * P
                 nc.tensor.matmul_mx(
@@ -178,58 +197,155 @@ def tile_contentaddressing_t_kernel(tc, memory, keys, betas, mask, out):
                     rhs=dat[:, g * CHUNK:(g + 1) * CHUNK].bitcast(FP8X4),
                     rhs_scale=scl[:, g * CHUNK:(g + 1) * CHUNK],
                     start=(g == 0), stop=(g == G - 1))
+            pr[(n, op)] = acc
 
-        def scores(k):
-            mc, ms, qc, qs = codes[k]
-            for t in range(HT):
-                c1 = slice(t, t + 1)
-                mn2 = psum.tile([P, CHUNK], F32, name="mn2")
-                product(mn2, t, 1, qc, qs)
-                dots = psum.tile([P, CHUNK], F32, name="dots")
-                product(dots, t, 0, mc, ms)
-                w = wrk.tile([P, CHUNK], F32, name="w")
-                nc.scalar.activation(out=w[:], in_=mn2[:], func=AF.Abs_reciprocal_sqrt,
-                                     bias=b1[:], scale=sc1[:, c1])
-                nc.vector.scalar_tensor_tensor(out=w[:], in0=w[:], scalar=1.0, in1=mn2[:],
-                                               op0=ALU.add, op1=ALU.mult)
-                nc.scalar.activation(out=w[:], in_=w[:], func=AF.Abs_reciprocal_sqrt,
-                                     bias=e2[:, c1], scale=1.0)
-                sc = s_all[t][:, k * CHUNK:(k + 1) * CHUNK]
-                nc.vector.scalar_tensor_tensor(out=sc, in0=dots[:], scalar=bk[:, c1], in1=w[:],
-                                               op0=ALU.mult, op1=ALU.mult)
-                if t == 0:
-                    nc.vector.tensor_reduce(out=mxp[:, k:k + 1], in_=sc, axis=AX.X, op=ALU.max)
+        def a1(n):
+            t = n % HT
+            w = wrk.tile([P, CHUNK], F32, name="w")
+            nc.scalar.activation(out=w[:], in_=pr[(n, 1)][:], func=AF.Abs_reciprocal_sqrt,
+                                 bias=b1[:], scale=sc1[:, t:t + 1])
+            pr[(n, "w")] = w
 
-        mem_prep(0)
-        for k in range(NCH):
-            if k + 2 < NCH:
-                load_mem(k + 2)
-            if k + 1 < NCH:
-                mem_prep(k + 1)
-            scores(k)
+        def v1(n):
+            w = pr[(n, "w")]
+            nc.vector.scalar_tensor_tensor(out=w[:], in0=w[:], scalar=1.0, in1=pr[(n, 1)][:],
+                                           op0=ALU.add, op1=ALU.mult)
+
+        def a2(n):
+            t = n % HT
+            w = pr[(n, "w")]
+            nc.scalar.activation(out=w[:], in_=w[:], func=AF.Abs_reciprocal_sqrt,
+                                 bias=e2[:, t:t + 1], scale=1.0)
+
+        def v2(n):
+            k, t = divmod(n, HT)
+            nc.vector.scalar_tensor_tensor(out=s_all[t][:, k * CHUNK:(k + 1) * CHUNK], in0=pr[(n, 0)][:],
+                                           scalar=bk[:, t:t + 1], in1=pr[(n, "w")][:],
+                                           op0=ALU.mult, op1=ALU.mult)
+
+        def max0(k):
+            nc.vector.tensor_reduce(out=mxp[:, k:k + 1], in_=s_all[0][:, k * CHUNK:(k + 1) * CHUNK],
+                                    axis=AX.X, op=ALU.max)
+
+        def mem_first(k):
+            mem_tiles(k)
+            for b in range(4):
+                mem_transposes(k, b)
+                mem_evac(k, b)
 
         for t in range(HT):
-            mrow = const.tile([P, 1], F32, name="mrow%d" % t)
-            nc.vector.tensor_reduce(out=mrow[:], in_=(mxp[:] if t == 0 else s_all[t][:]), axis=AX.X, op=ALU.max)
-            negm = const.tile([P, 1], F32, name="negm%d" % t)
-            nc.vector.tensor_scalar(out=negm[:], in0=mrow[:], scalar1=-1.0, scalar2=None, op0=ALU.mult)
-            sums = const.tile([P, 2], F32, name="sums%d" % t)
-            for i in range(2):
-                cs = slice(i * 2048, (i + 1) * 2048)
-                nc.scalar.activation(out=s_all[t][:, cs], in_=s_all[t][:, cs], func=AF.Exp,
-                                     bias=negm[:], scale=1.0, accum_out=sums[:, i:i + 1])
-            tot = const.tile([P, 1], F32, name="tot%d" % t)
-            nc.vector.tensor_reduce(out=tot[:], in_=sums[:], axis=AX.X, op=ALU.add)
-            rs = const.tile([P, 1], F32, name="rs%d" % t)
-            nc.vector.reciprocal(out=rs[:], in_=tot[:])
-            for q in range(4):
-                cs = slice(q * 1024, (q + 1) * 1024)
-                piece = s_all[t][:, cs]
-                if t == HT - 1 and q < 2:
-                    nc.vector.tensor_scalar(out=piece, in0=piece, scalar1=rs[:], scalar2=None, op0=ALU.mult)
-                elif t == HT - 1 and q == 2:
-                    nc.scalar.activation(out=piece, in_=piece, func=AF.Copy, scale=rs[:])
-                else:
-                    nc.gpsimd.tensor_scalar(out=piece, in0=piece, scalar1=rs[:], scalar2=0.0,
-                                            op0=ALU.mult, op1=ALU.add)
-                nc.sync.dma_start(out=out2d[t * P:(t + 1) * P, cs], in_=piece)
+            key_square(t)
+        key_products(0)
+        key_transposes(0, 1)
+        key_transposes(1, 1)
+        key_evac(0, 1, "a")
+        key_evac(1, 1, "a")
+        key_products(1)
+        key_transposes(2, 1)
+        key_transposes(3, 1)
+        key_evac(2, 1, "a")
+        key_evac(3, 1, "a")
+        key_products(2)
+        key_transposes(0, 0)
+        key_transposes(1, 0)
+        key_evac(0, 0, "a")
+        key_evac(1, 0, "a")
+        key_products(3)
+        nc.scalar.activation(out=rk[:], in_=kn2[:], func=AF.Abs_reciprocal_sqrt, bias=tiny[:], scale=1.0)
+        key_transposes(2, 0)
+        key_transposes(3, 0)
+        mem_first(0)
+        key_evac(2, 0, "v")
+        key_quant(0)
+        key_evac(3, 0, "v")
+        key_quant(1)
+        key_quant(2)
+        key_quant(3)
+        nc.vector.tensor_scalar(out=sc1[:], in0=kn2[:], scalar1=1.0 / (4.0 * EPS * EPS),
+                                scalar2=3e38, op0=ALU.mult, op1=ALU.min)
+        nc.vector.tensor_tensor(out=rk2[:], in0=rk[:], in1=rk[:], op=ALU.mult)
+        nc.vector.tensor_scalar(out=e2[:], in0=rk2[:], scalar1=EPS * EPS,
+                                scalar2=1e-37, op0=ALU.mult, op1=ALU.max)
+        nc.vector.tensor_tensor(out=bk[:], in0=beta_f[:], in1=rk[:], op=ALU.mult)
+        mem_square_vec(0)
+        quant(0, "msq")
+        mem_first(1)
+        product(0, 1)
+        quant(0, "mgrp")
+        product(0, 0)
+        for b in range(LEAD):
+            mem_transposes(2, b)
+
+        for n in range(NPAIR + 1):
+            k, j = divmod(n, HT)
+            if j == 0 and k + 3 < NCH:
+                load_mem(k + 3)
+            if n + 1 < NPAIR:
+                product(n + 1, 1)
+            if n < NPAIR:
+                a1(n)
+                v1(n)
+            if n >= 1:
+                a2(n - 1)
+                v2(n - 1)
+            if n + 1 < NPAIR:
+                product(n + 1, 0)
+            ka, ba = divmod(n + LEAD, HT)
+            if ka + 2 < NCH:
+                mem_transposes(ka + 2, ba)
+            if k + 2 < NCH:
+                if j == 0:
+                    mem_tiles(k + 2)
+                mem_evac(k + 2, j)
+            if k + 1 < NCH:
+                if j == 0:
+                    mem_square_vec(k + 1)
+                elif j == 1:
+                    quant(k + 1, "msq")
+                elif j == 2:
+                    quant(k + 1, "mgrp")
+            if j == 3:
+                max0(k)
+
+        negm = [const.tile([P, 1], F32, name="negm%d" % t) for t in range(HT)]
+        mrow = [const.tile([P, 1], F32, name="mrow%d" % t) for t in range(HT)]
+        sums = [const.tile([P, 1], F32, name="sums%d" % t) for t in range(HT)]
+        rs = [const.tile([P, 1], F32, name="rs%d" % t) for t in range(HT)]
+
+        def row_max(t):
+            nc.vector.tensor_reduce(out=mrow[t][:], in_=(mxp[:] if t == 0 else s_all[t][:]), axis=AX.X, op=ALU.max)
+            nc.vector.tensor_scalar(out=negm[t][:], in0=mrow[t][:], scalar1=-1.0, scalar2=None, op0=ALU.mult)
+
+        def row_exp(t):
+            nc.scalar.activation(out=s_all[t][:], in_=s_all[t][:], func=AF.Exp,
+                                 bias=negm[t][:], scale=1.0, accum_out=sums[t][:])
+
+        def row_recip(t):
+            nc.vector.reciprocal(out=rs[t][:], in_=sums[t][:])
+
+        def row_scale_store(t, q, eng):
+            cs = slice(q * 1024, (q + 1) * 1024)
+            piece = s_all[t][:, cs]
+            if eng == "v":
+                nc.vector.tensor_scalar(out=piece, in0=piece, scalar1=rs[t][:], scalar2=None, op0=ALU.mult)
+            elif eng == "a":
+                nc.scalar.activation(out=piece, in_=piece, func=AF.Copy, scale=rs[t][:])
+            else:
+                nc.gpsimd.tensor_scalar(out=piece, in0=piece, scalar1=rs[t][:], scalar2=0.0,
+                                        op0=ALU.mult, op1=ALU.add)
+            nc.sync.dma_start(out=out2d[t * P:(t + 1) * P, cs], in_=piece)
+
+        row_max(0)
+        row_exp(0)
+        row_max(1)
+        for t in range(HT):
+            if t + 1 < HT:
+                row_exp(t + 1)
+            row_recip(t)
+            last = t == HT - 1
+            row_scale_store(t, 0, "v")
+            row_scale_store(t, 1, "v" if last else "g")
+            row_scale_store(t, 2, "a" if last else "g")
+            row_scale_store(t, 3, "g")
+            if t + 2 < HT:
+                row_max(t + 2)

@@ -20,6 +20,8 @@ NCH = C // CHUNK
 G = W // 512
 NPAIR = NCH * HT
 LEAD = 2
+ACT_BLOCKS = (1, 1, 1, 0)
+VEC_RUNS = ((0, 3, 1), (3, 4, 0),)
 EPS = 1e-8
 FLOPS = 2 * 2 * H * C * W
 
@@ -164,16 +166,20 @@ def tile_contentaddressing_t_kernel(tc, memory, keys, betas, mask, out):
             tb = mp[(k, "tb", b)]
             nc.scalar.copy(out=mp[(k, "mgrp")][:].bitcast(F32)[:, g, 256 * half:256 * half + 256, :],
                            in_=tb[:].rearrange("p u r -> p r u"))
-            nc.scalar.activation(
-                out=mp[(k, "msq")][:, g, 256 * half:256 * half + P, :].rearrange("p r (u e) -> p r u e", e=2),
-                in_=tb[:, :, 0:P].bitcast(BF16).rearrange("p u (r e) -> p r u e", e=2),
-                func=AF.Square)
+            n_act = ACT_BLOCKS[b] * P
+            if n_act:
+                nc.scalar.activation(
+                    out=mp[(k, "msq")][:, g, 256 * half:256 * half + n_act, :].rearrange("p r (u e) -> p r u e", e=2),
+                    in_=tb[:, :, 0:n_act].bitcast(BF16).rearrange("p u (r e) -> p r u e", e=2),
+                    func=AF.Square)
 
         def mem_square_vec(k):
             view = "p g (h j c) s -> p (g h) j (c s)"
-            src = mp[(k, "mgrp")][:].rearrange(view, h=2, j=2, c=P)[:, :, 1, :]
-            dst = mp[(k, "msq")][:].rearrange(view, h=2, j=2, c=P)[:, :, 1, :]
-            nc.vector.tensor_tensor(out=dst, in0=src, in1=src, op=ALU.mult)
+            src = mp[(k, "mgrp")][:].rearrange(view, h=2, j=2, c=P)
+            dst = mp[(k, "msq")][:].rearrange(view, h=2, j=2, c=P)
+            for b0, b1, j0 in VEC_RUNS:
+                nc.vector.tensor_tensor(out=dst[:, b0:b1, j0:2, :], in0=src[:, b0:b1, j0:2, :],
+                                        in1=src[:, b0:b1, j0:2, :], op=ALU.mult)
 
         def quant(k, which):
             dat = cod.tile([P, G * CHUNK], U32, name="dat_" + which, align_bytes=64)

@@ -20,8 +20,8 @@ NCH = C // CHUNK
 G = W // 512
 NPAIR = NCH * HT
 LEAD = 2
-ACT_BLOCKS = (1, 1, 1, 0)
-VEC_RUNS = ((0, 3, 1), (3, 4, 0),)
+ACT_BLOCKS = (1, 1, 0, 0)
+VEC_RUNS = ((0, 2, 1), (2, 4, 0),)
 EPS = 1e-8
 FLOPS = 2 * 2 * H * C * W
 

@@ -20,8 +20,8 @@ NCH = C // CHUNK
 G = W // 512
 NPAIR = NCH * HT
 LEAD = 2
-ACT_BLOCKS = (1, 1, 0, 0)
-VEC_RUNS = ((0, 2, 1), (2, 4, 0),)
+ACT_BLOCKS = (1, 1, 1, 0)
+VEC_RUNS = ((0, 3, 1), (3, 4, 0),)
 EPS = 1e-8
 FLOPS = 2 * 2 * H * C * W
 
@@ -178,8 +178,11 @@ def tile_contentaddressing_t_kernel(tc, memory, keys, betas, mask, out):
             src = mp[(k, "mgrp")][:].rearrange(view, h=2, j=2, c=P)
             dst = mp[(k, "msq")][:].rearrange(view, h=2, j=2, c=P)
             for b0, b1, j0 in VEC_RUNS:
-                nc.vector.tensor_tensor(out=dst[:, b0:b1, j0:2, :], in0=src[:, b0:b1, j0:2, :],
-                                        in1=src[:, b0:b1, j0:2, :], op=ALU.mult)
+                if k == NCH - 1:
+                    nc.scalar.activation(out=dst[:, b0:b1, j0:2, :], in_=src[:, b0:b1, j0:2, :], func=AF.Square)
+                else:
+                    nc.vector.tensor_tensor(out=dst[:, b0:b1, j0:2, :], in0=src[:, b0:b1, j0:2, :],
+                                            in1=src[:, b0:b1, j0:2, :], op=ALU.mult)
 
         def quant(k, which):
             dat = cod.tile([P, G * CHUNK], U32, name="dat_" + which, align_bytes=64)

@@ -20,8 +20,9 @@ NCH = C // CHUNK
 G = W // 512
 NPAIR = NCH * HT
 LEAD = 2
-ACT_BLOCKS = (1, 1, 1, 0)
-VEC_RUNS = ((0, 3, 1), (3, 4, 0),)
+ACT_BLOCKS = (0, 1, 1, 0)
+VEC_RUNS = ((1, 3, 1), (3, 4, 0),)
+POOL_PIECES = 4
 EPS = 1e-8
 FLOPS = 2 * 2 * H * C * W
 
@@ -166,6 +167,13 @@ def tile_contentaddressing_t_kernel(tc, memory, keys, betas, mask, out):
             tb = mp[(k, "tb", b)]
             nc.scalar.copy(out=mp[(k, "mgrp")][:].bitcast(F32)[:, g, 256 * half:256 * half + 256, :],
                            in_=tb[:].rearrange("p u r -> p r u"))
+            if b == 0:
+                step = 256 // POOL_PIECES
+                for i in range(POOL_PIECES):
+                    src = mp[(k, "mgrp")][:, 0, i * step:(i + 1) * step, :].rearrange("p c s -> p (c s)")
+                    nc.gpsimd.tensor_tensor(
+                        out=mp[(k, "msq")][:, 0, i * step:(i + 1) * step, :].rearrange("p c s -> p (c s)"),
+                        in0=src, in1=src, op=ALU.mult)
             n_act = ACT_BLOCKS[b] * P
             if n_act:
                 nc.scalar.activation(
@@ -178,11 +186,8 @@ def tile_contentaddressing_t_kernel(tc, memory, keys, betas, mask, out):
             src = mp[(k, "mgrp")][:].rearrange(view, h=2, j=2, c=P)
             dst = mp[(k, "msq")][:].rearrange(view, h=2, j=2, c=P)
             for b0, b1, j0 in VEC_RUNS:
-                if k == NCH - 1:
-                    nc.scalar.activation(out=dst[:, b0:b1, j0:2, :], in_=src[:, b0:b1, j0:2, :], func=AF.Square)
-                else:
-                    nc.vector.tensor_tensor(out=dst[:, b0:b1, j0:2, :], in0=src[:, b0:b1, j0:2, :],
-                                            in1=src[:, b0:b1, j0:2, :], op=ALU.mult)
+                nc.vector.tensor_tensor(out=dst[:, b0:b1, j0:2, :], in0=src[:, b0:b1, j0:2, :],
+                                        in1=src[:, b0:b1, j0:2, :], op=ALU.mult)
 
         def quant(k, which):
             dat = cod.tile([P, G * CHUNK], U32, name="dat_" + which, align_bytes=64)

from contextlib import ExitStack

import concourse.mybir as mybir
from concourse.masks import make_identity

F32 = mybir.dt.float32
BF16 = mybir.dt.bfloat16
U32 = mybir.dt.uint32
U8 = mybir.dt.uint8
FP8X4 = mybir.dt.float8_e4m3fn_x4
AF = mybir.ActivationFunctionType
ALU = mybir.AluOpType
AX = mybir.AxisListType

P = 128
H, C, W = 512, 4096, 1024
HT = H // P
CHUNK = 512
NCH = C // CHUNK
G = W // 512
NPAIR = NCH * HT
LEAD = 2
ACT_BLOCKS = (0, 1, 1, 0)
VEC_RUNS = ((1, 3, 1), (3, 4, 0),)
POOL_PIECES = 4
EPS = 1e-8
FLOPS = 2 * 2 * H * C * W


def tile_contentaddressing_t_kernel(tc, memory, keys, betas, mask, out):
    nc = tc.nc
    mem2d = memory.flatten_outer_dims()
    keys2d = keys.flatten_outer_dims()
    mask2d = mask.flatten_outer_dims()
    out2d = out.flatten_outer_dims()

    with ExitStack() as ctx:
        const = ctx.enter_context(tc.tile_pool(name="const", bufs=1))
        natp = ctx.enter_context(tc.tile_pool(name="natp", bufs=3))
        grp = ctx.enter_context(tc.tile_pool(name="grp", bufs=2))
        cod = ctx.enter_context(tc.tile_pool(name="cod", bufs=3))
        wrk = ctx.enter_context(tc.tile_pool(name="wrk", bufs=4))
        psum = ctx.enter_context(tc.psum_pool(name="psum", bufs=2))
        ctx.enter_context(tc.manual_schedule())

        tiny = const.tile([P, 1], F32, name="tiny")
        nc.vector.memset(tiny[:], 1e-30)
        b1 = const.tile([P, 1], F32, name="b1")
        nc.vector.memset(b1[:], 1e-16)
        warm = const.tile([P, 1], F32, name="warm")
        nc.scalar.activation(out=warm[:], in_=b1[:], func=AF.Abs_reciprocal_sqrt, bias=tiny[:], scale=1.0)
        brow = const.tile([P, P], BF16, name="brow")
        nc.vector.memset(brow[:], 0.0)
        ident_f = const.tile([P, P], F32, name="ident_f")
        make_identity(nc, ident_f[:])
        ident_b = const.tile([P, P], BF16, name="ident_b")
        make_identity(nc, ident_b[:])

        keys_nat = const.tile([P, HT, W], BF16, name="keys_nat")
        mask_nat = const.tile([P, HT, W], BF16, name="mask_nat")
        kview = keys2d.rearrange("(t p) w -> p t w", p=P)
        mview = mask2d.rearrange("(t p) w -> p t w", p=P)
        nat = {}

        def load_mem(k):
            t_nat = natp.tile([P, 4, W], BF16, name="mem_nat")
            nc.sync.dma_start(
                out=t_nat[:],
                in_=mem2d[k * CHUNK:(k + 1) * CHUNK, :].rearrange("(j p) w -> p j w", p=P),
            )
            nat[k] = t_nat

        nc.scalar.dma_start(out=brow[0:HT, :], in_=betas.rearrange("o (t p) -> (o t) p", p=P))
        for t in range(HT):
            nc.sync.dma_start(out=mask_nat[:, t, :], in_=mview[:, t, :])
            nc.sync.dma_start(out=keys_nat[:, t, :], in_=kview[:, t, :])
        load_mem(0)
        load_mem(1)
        load_mem(2)

        beta_f = const.tile([P, HT], F32, name="beta_f")
        kn2 = const.tile([P, HT], F32, name="kn2")
        rk = const.tile([P, HT], F32, name="rk")
        rk2 = const.tile([P, HT], F32, name="rk2")
        sc1 = const.tile([P, HT], F32, name="sc1")
        e2 = const.tile([P, HT], F32, name="e2")
        bk = const.tile([P, HT], F32, name="bk")
        kcodes = const.tile([P, HT * 512], U32, name="kcodes", align_bytes=64)
        kscale = const.tile([P, HT * 512], U8, name="kscale", align_bytes=64)
        kgrp = [const.tile([P, 2, G, P, 4], BF16, name="kgrp%d" % t, align_bytes=64) for t in range(HT)]
        s_all = [const.tile([P, C], F32, name="s%d" % t) for t in range(HT)]
        mxp = const.tile([P, NCH], F32, name="mxp")

        def t_bank(shape, dtype):
            return psum.tile(shape, dtype, name="tbank", tag="T", bufs=3)

        def acc_bank(op, shape):
            if op == 0:
                return psum.tile(shape, F32, name="dots", tag="dots", bufs=3)
            return psum.tile(shape, F32, name="mn2", tag="mn2", bufs=2)

        bT = t_bank([P, P], BF16)
        nc.tensor.transpose(out=bT[:], in_=brow[:], identity=ident_b[:])
        nc.vector.tensor_copy(out=beta_f[:], in_=bT[:, 0:HT])

        perm = "p (a q e) -> p a e q"
        m2f = [s_all[t][:, 0:W] for t in range(HT)]
        km2f = [s_all[t][:, W:2 * W] for t in range(HT)]
        junk = [s_all[t][:, 2 * W:3 * W] for t in range(HT)]
        kx = {}

        def key_square(t):
            nc.scalar.activation(out=m2f[t], in_=mask_nat[:, t, :], func=AF.Square)

        def key_products(t):
            k_t = keys_nat[:, t, :]
            nc.vector.tensor_tensor(out=km2f[t], in0=k_t, in1=m2f[t], op=ALU.mult)
            nc.vector.scalar_tensor_tensor(out=junk[t], in0=k_t, scalar=1.0, in1=km2f[t],
                                           op0=ALU.mult, op1=ALU.mult, accum_out=kn2[:, t:t + 1])

        def key_transposes(t, op):
            cols = (km2f[t] if op == 0 else m2f[t]).rearrange(perm, a=4, q=P, e=2)
            for g in range(G):
                xt = acc_bank(g, [P, 4, P])
                for u in range(2):
                    for e in range(2):
                        nc.tensor.transpose(out=xt[:, 2 * u + e, :], in_=cols[:, 2 * g + u, e, :],
                                            identity=ident_f[:])
                kx[(t, op, g)] = xt

        def key_evac(t, op, eng):
            for g in range(G):
                src = kx[(t, op, g)][:].rearrange("p s h -> p h s")
                if eng == "v":
                    nc.vector.tensor_copy(out=kgrp[t][:, op, g], in_=src)
                else:
                    nc.scalar.copy(out=kgrp[t][:, op, g], in_=src)

        def key_quant(t):
            nc.vector.quantize_mx(
                out=kcodes[:, t * 512:(t + 1) * 512].bitcast(FP8X4),
                scales=kscale[:, t * 512:(t + 1) * 512],
                in_=kgrp[t][:].rearrange("p o g h s -> p (o g h s)"),
            )

        mp = {}

        def mem_transposes(k, b):
            g, half = divmod(b, 2)
            memf = nat[k][:].bitcast(F32)
            tb = t_bank([P, 2, 256], F32)
            for jj in range(2):
                for u in range(2):
                    i = 2 * g + u
                    nc.tensor.transpose(
                        out=tb[:, u, jj * P:(jj + 1) * P],
                        in_=memf[:, 2 * half + jj, i * P:(i + 1) * P],
                        identity=ident_f[:])
            mp[(k, "tb", b)] = tb

        def mem_tiles(k):
            mp[(k, "mgrp")] = grp.tile([P, G, CHUNK, 4], BF16, name="mgrp", align_bytes=64)
            mp[(k, "msq")] = grp.tile([P, G, CHUNK, 4], BF16, name="msq", align_bytes=64)

        def mem_evac(k, b):
            g, half = divmod(b, 2)
            tb = mp[(k, "tb", b)]
            nc.scalar.copy(out=mp[(k, "mgrp")][:].bitcast(F32)[:, g, 256 * half:256 * half + 256, :],
                           in_=tb[:].rearrange("p u r -> p r u"))
            if b == 0:
                step = 256 // POOL_PIECES
                for i in range(POOL_PIECES):
                    src = mp[(k, "mgrp")][:, 0, i * step:(i + 1) * step, :].rearrange("p c s -> p (c s)")
                    nc.gpsimd.tensor_tensor(
                        out=mp[(k, "msq")][:, 0, i * step:(i + 1) * step, :].rearrange("p c s -> p (c s)"),
                        in0=src, in1=src, op=ALU.mult)
            n_act = ACT_BLOCKS[b] * P
            if n_act:
                nc.scalar.activation(
                    out=mp[(k, "msq")][:, g, 256 * half:256 * half + n_act, :].rearrange("p r (u e) -> p r u e", e=2),
                    in_=tb[:, :, 0:n_act].bitcast(BF16).rearrange("p u (r e) -> p r u e", e=2),
                    func=AF.Square)

        def mem_square_vec(k):
            view = "p g (h j c) s -> p (g h) j (c s)"
            src = mp[(k, "mgrp")][:].rearrange(view, h=2, j=2, c=P)
            dst = mp[(k, "msq")][:].rearrange(view, h=2, j=2, c=P)
            for b0, b1, j0 in VEC_RUNS:
                nc.vector.tensor_tensor(out=dst[:, b0:b1, j0:2, :], in0=src[:, b0:b1, j0:2, :],
                                        in1=src[:, b0:b1, j0:2, :], op=ALU.mult)

        def quant(k, which):
            dat = cod.tile([P, G * CHUNK], U32, name="dat_" + which, align_bytes=64)
            scl = cod.tile([P, G * CHUNK], U8, name="scl_" + which, align_bytes=64)
            nc.vector.quantize_mx(out=dat[:].bitcast(FP8X4), scales=scl[:],
                                  in_=mp[(k, which)][:].rearrange("p g c s -> p (g c s)"))
            mp[(k, "q", which)] = (dat, scl)

        pr = {}

        def product(n, op):
            k, t = divmod(n, HT)
            acc = acc_bank(op, [P, CHUNK])
            dat, scl = mp[(k, "q", "mgrp" if op == 0 else "msq")]
            for g in range(G):
                c0 = t * 512 + (op * G + g) * P
                nc.tensor.matmul_mx(
                    out=acc[:],
                    lhsT=kcodes[:, c0:c0 + P].bitcast(FP8X4),
                    lhsT_scale=kscale[:, c0:c0 + P],
                    rhs=dat[:, g * CHUNK:(g + 1) * CHUNK].bitcast(FP8X4),
                    rhs_scale=scl[:, g * CHUNK:(g + 1) * CHUNK],
                    start=(g == 0), stop=(g == G - 1))
            pr[(n, op)] = acc

        def a1(n):
            t = n % HT
            w = wrk.tile([P, CHUNK], F32, name="w")
            nc.scalar.activation(out=w[:], in_=pr[(n, 1)][:], func=AF.Abs_reciprocal_sqrt,
                                 bias=b1[:], scale=sc1[:, t:t + 1])
            pr[(n, "w")] = w

        def v1(n):
            w = pr[(n, "w")]
            nc.vector.scalar_tensor_tensor(out=w[:], in0=w[:], scalar=1.0, in1=pr[(n, 1)][:],
                                           op0=ALU.add, op1=ALU.mult)

        def a2(n):
            t = n % HT
            w = pr[(n, "w")]
            nc.scalar.activation(out=w[:], in_=w[:], func=AF.Abs_reciprocal_sqrt,
                                 bias=e2[:, t:t + 1], scale=1.0)

        def v2(n):
            k, t = divmod(n, HT)
            nc.vector.scalar_tensor_tensor(out=s_all[t][:, k * CHUNK:(k + 1) * CHUNK], in0=pr[(n, 0)][:],
                                           scalar=bk[:, t:t + 1], in1=pr[(n, "w")][:],
                                           op0=ALU.mult, op1=ALU.mult)

        def max0(k):
            nc.vector.tensor_reduce(out=mxp[:, k:k + 1], in_=s_all[0][:, k * CHUNK:(k + 1) * CHUNK],
                                    axis=AX.X, op=ALU.max)

        def mem_first(k):
            mem_tiles(k)
            for b in range(4):
                mem_transposes(k, b)
                mem_evac(k, b)

        for t in range(HT):
            key_square(t)
        key_products(0)
        key_transposes(0, 1)
        key_transposes(1, 1)
        key_evac(0, 1, "a")
        key_evac(1, 1, "a")
        key_products(1)
        key_transposes(2, 1)
        key_transposes(3, 1)
        key_evac(2, 1, "a")
        key_evac(3, 1, "a")
        key_products(2)
        key_transposes(0, 0)
        key_transposes(1, 0)
        key_evac(0, 0, "a")
        key_evac(1, 0, "a")
        key_products(3)
        nc.scalar.activation(out=rk[:], in_=kn2[:], func=AF.Abs_reciprocal_sqrt, bias=tiny[:], scale=1.0)
        key_transposes(2, 0)
        key_transposes(3, 0)
        mem_first(0)
        key_evac(2, 0, "v")
        key_quant(0)
        key_evac(3, 0, "v")
        key_quant(1)
        key_quant(2)
        key_quant(3)
        nc.vector.tensor_scalar(out=sc1[:], in0=kn2[:], scalar1=1.0 / (4.0 * EPS * EPS),
                                scalar2=3e38, op0=ALU.mult, op1=ALU.min)
        nc.vector.tensor_tensor(out=rk2[:], in0=rk[:], in1=rk[:], op=ALU.mult)
        nc.vector.tensor_scalar(out=e2[:], in0=rk2[:], scalar1=EPS * EPS,
                                scalar2=1e-37, op0=ALU.mult, op1=ALU.max)
        nc.vector.tensor_tensor(out=bk[:], in0=beta_f[:], in1=rk[:], op=ALU.mult)
        mem_square_vec(0)
        quant(0, "msq")
        mem_first(1)
        product(0, 1)
        quant(0, "mgrp")
        product(0, 0)
        for b in range(LEAD):
            mem_transposes(2, b)

        for n in range(NPAIR + 1):
            k, j = divmod(n, HT)
            if j == 0 and k + 3 < NCH:
                load_mem(k + 3)
            if n + 1 < NPAIR:
                product(n + 1, 1)
            if n < NPAIR:
                a1(n)
                v1(n)
            if n >= 1:
                a2(n - 1)
                v2(n - 1)
            if n + 1 < NPAIR:
                product(n + 1, 0)
            ka, ba = divmod(n + LEAD, HT)
            if ka + 2 < NCH:
                mem_transposes(ka + 2, ba)
            if k + 2 < NCH:
                if j == 0:
                    mem_tiles(k + 2)
                mem_evac(k + 2, j)
            if k + 1 < NCH:
                if j == 0:
                    mem_square_vec(k + 1)
                elif j == 1:
                    quant(k + 1, "msq")
                elif j == 2:
                    quant(k + 1, "mgrp")
            if j == 3:
                max0(k)

        negm = [const.tile([P, 1], F32, name="negm%d" % t) for t in range(HT)]
        mrow = [const.tile([P, 1], F32, name="mrow%d" % t) for t in range(HT)]
        sums = [const.tile([P, 1], F32, name="sums%d" % t) for t in range(HT)]
        rs = [const.tile([P, 1], F32, name="rs%d" % t) for t in range(HT)]

        def row_max(t):
            nc.vector.tensor_reduce(out=mrow[t][:], in_=(mxp[:] if t == 0 else s_all[t][:]), axis=AX.X, op=ALU.max)
            nc.vector.tensor_scalar(out=negm[t][:], in0=mrow[t][:], scalar1=-1.0, scalar2=None, op0=ALU.mult)

        def row_exp(t):
            nc.scalar.activation(out=s_all[t][:], in_=s_all[t][:], func=AF.Exp,
                                 bias=negm[t][:], scale=1.0, accum_out=sums[t][:])

        def row_recip(t):
            nc.vector.reciprocal(out=rs[t][:], in_=sums[t][:])

        def row_scale_store(t, q, eng):
            cs = slice(q * 1024, (q + 1) * 1024)
            piece = s_all[t][:, cs]
            if eng == "v":
                nc.vector.tensor_scalar(out=piece, in0=piece, scalar1=rs[t][:], scalar2=None, op0=ALU.mult)
            elif eng == "a":
                nc.scalar.activation(out=piece, in_=piece, func=AF.Copy, scale=rs[t][:])
            else:
                nc.gpsimd.tensor_scalar(out=piece, in0=piece, scalar1=rs[t][:], scalar2=0.0,
                                        op0=ALU.mult, op1=ALU.add)
            nc.sync.dma_start(out=out2d[t * P:(t + 1) * P, cs], in_=piece)

        row_max(0)
        row_exp(0)
        row_max(1)
        for t in range(HT):
            if t + 1 < HT:
                row_exp(t + 1)
            row_recip(t)
            last = t == HT - 1
            row_scale_store(t, 0, "v")
            row_scale_store(t, 1, "v" if last else "g")
            row_scale_store(t, 2, "a" if last else "g")
            row_scale_store(t, 3, "g")
            if t + 2 < HT:
                row_max(t + 2)
